import numpy as np
import ml_dtypes


def mxq(x, axis, fmt="e4m3"):
    dtype, down = {"e4m3": (ml_dtypes.float8_e4m3fn, 7), "e5m2": (ml_dtypes.float8_e5m2, 14)}[fmt]
    v = np.moveaxis(np.asarray(x, np.float32).astype(ml_dtypes.bfloat16).astype(np.float64), axis, -1)
    blocks = v.reshape(v.shape[:-1] + (-1, 32))
    amax = np.abs(blocks).max(-1, keepdims=True)
    byte = np.maximum(np.where(amax > 0, np.frexp(amax)[1] - 1 + 127, 0) - down, 1)
    scale = np.exp2(byte - 127.0)
    codes = (blocks / scale).astype(np.float32).astype(dtype).astype(np.float64)
    return np.moveaxis((codes * scale).reshape(v.shape), -1, axis)


WIDE = False


def mx_kscale(k):
    if not WIDE:
        return np.ones(k)
    levels = np.array([10, -10, 5, -5, 0])
    a = np.random.permutation(np.resize(levels, k // 512 * 4)).reshape(k // 512, 4)
    idx = np.arange(k)
    return np.exp2(a[idx // 512, idx % 128 // 32])


BF16 = ml_dtypes.bfloat16


def bf(x):
    return np.asarray(x, np.float32).astype(BF16)


def f64(x):
    return np.asarray(x).astype(np.float64)


B, T, N, D, L = 1, 8, 128, 1024, 512


def setup_inputs():
    s, r = mx_kscale(D), mx_kscale(L)
    x = np.random.standard_normal((B, T, N, D)) + 0.5 * np.random.standard_normal(D)
    return {"x": bf(x * s),
            "Wtheta": bf(np.random.standard_normal((L, D)) / np.sqrt(D) / s * r[:, None]),
            "Wphi": bf(np.random.standard_normal((L, D)) / np.sqrt(D) / s / r[:, None])}


def reference(x, Wtheta, Wphi):
    xq = mxq(f64(x), 3, "e4m3")
    th = xq @ mxq(f64(Wtheta), 1, "e4m3").T
    ph = xq @ mxq(f64(Wphi), 1, "e4m3").T
    thq, phq = mxq(th, 3, "e4m3"), mxq(ph, 3, "e4m3")
    sw = (thq @ phq.transpose(0, 1, 3, 2)) / N
    tw = (thq.transpose(0, 2, 1, 3) @ phq.transpose(0, 2, 3, 1)).transpose(0, 2, 1, 3) / T
    return sw, tw

@@ -1,0 +1,218 @@
+from contextlib import ExitStack
+
+import concourse.mybir as mybir
+from concourse.masks import make_identity
+
+F32 = mybir.dt.float32
+BF16 = mybir.dt.bfloat16
+U32 = mybir.dt.uint32
+I32 = mybir.dt.int32
+U8 = mybir.dt.uint8
+FP8X4 = mybir.dt.float8_e4m3fn_x4
+ALU = mybir.AluOpType
+AX = mybir.AxisListType
+
+P = 128
+T = 8
+N = 128
+D = 1024
+L = 512
+FLOPS = 2 * (T * N) * D * (2 * L) + 2 * T * N * N * L + 2 * N * T * T * L
+
+W_EXIT = ("s", "v", "s", "v")
+X_EXIT = ("s", "v", "s", "v", "s", "s", "s", "s")
+
+
+def tile_higcin_volleyball_pa_kernel(tc, x, Wtheta, Wphi, out_0, out_1):
+    nc = tc.nc
+    with ExitStack() as ctx:
+        raw = ctx.enter_context(tc.tile_pool(name="raw", bufs=1))
+        keep = ctx.enter_context(tc.tile_pool(name="keep", bufs=1))
+        stage = ctx.enter_context(tc.tile_pool(name="stage", bufs=4))
+        tp_pool = ctx.enter_context(tc.psum_pool(name="tp", bufs=3))
+        mm_pool = ctx.enter_context(tc.psum_pool(name="mm", bufs=4))
+        sw_pool = ctx.enter_context(tc.psum_pool(name="swp", bufs=1))
+
+        w_dram = (
+            Wtheta.rearrange("(p t) d -> p t d", t=4),
+            Wphi.rearrange("(p t) d -> p t d", t=4),
+        )
+        w_raw = [[raw.tile([P, D], BF16, name="wraw%d_%d" % (w, t)) for t in range(4)] for w in range(2)]
+        x_raw = [raw.tile([P, D], BF16, name="xraw%d" % f) for f in range(T)]
+
+        def load_w(w):
+            for t in range(4):
+                nc.sync.dma_start(out=w_raw[w][t][:], in_=w_dram[w][:, t, :])
+
+        def load_x(f):
+            nc.sync.dma_start(out=x_raw[f][:], in_=x[0, f])
+
+        load_w(0)
+        load_x(0)
+        load_x(1)
+        load_w(1)
+        for f in range(2, T):
+            load_x(f)
+
+        ident = keep.tile([P, P], F32, name="ident")
+        make_identity(nc, ident[:])
+        m16raw = keep.tile([P, 16], F32, name="m16raw")
+        nc.vector.tensor_reduce(
+            out=m16raw[:], in_=ident[:].rearrange("p (t j) -> p j t", j=16), axis=AX.X, op=ALU.add
+        )
+        m16 = keep.tile([P, 16], F32, name="m16")
+        nc.vector.tensor_scalar_mul(out=m16[:], in0=m16raw[:], scalar1=1.0 / T)
+
+        wq = [[keep.tile([P, 256], U32, name="wq%d_%d" % (w, t), align_bytes=64) for t in range(4)] for w in range(2)]
+        ws = [[keep.tile([P, 256], U8, name="ws%d_%d" % (w, t), align_bytes=64) for t in range(4)] for w in range(2)]
+        xq = [keep.tile([P, 256], U32, name="xq%d" % f, align_bytes=64) for f in range(T)]
+        xs = [keep.tile([P, 256], U8, name="xs%d" % f, align_bytes=64) for f in range(T)]
+        hq = [keep.tile([P, 256], U32, name="hq%d" % f, align_bytes=64) for f in range(T)]
+        hs = [keep.tile([P, 256], U8, name="hs%d" % f, align_bytes=64) for f in range(T)]
+        for f in range(T):
+            nc.vector.memset(hs[f][:].bitcast(I32), 0)
+        tq = keep.tile([P, 2048], U32, name="tq", align_bytes=64)
+        ts = keep.tile([P, 2048], U8, name="ts", align_bytes=64)
+        tq_v = tq[:].bitcast(I32).rearrange("p (g w t j) -> p g w t j", g=8, w=2, t=T)
+        ts_v = ts[:].bitcast(I32).rearrange("p (g w t j) -> p g w t j", g=8, w=2, t=T)
+
+        def transposed(src, codes, scales, eng):
+            bank = tp_pool.tile([P, 2, 2, P], F32, tag="tp", name="bank")
+            words = src[:].bitcast(F32)
+            for g in range(2):
+                for u in range(2):
+                    c0 = 256 * g + 128 * u
+                    nc.tensor.transpose(bank[:, g, u, :], words[:, c0 : c0 + 128], ident[:])
+            grouped = stage.tile([P, 4 * 256], BF16, tag="grouped", name="grouped", align_bytes=64)
+            dst = grouped[:].bitcast(F32).rearrange("p (g r u) -> p g r u", g=2, u=2)
+            srcv = bank[:].rearrange("p g u r -> p g r u")
+            if eng == "s":
+                nc.scalar.copy(out=dst, in_=srcv)
+            else:
+                nc.vector.tensor_copy(out=dst, in_=srcv)
+            nc.vector.quantize_mx(out=codes[:].bitcast(FP8X4), scales=scales[:], in_=grouped[:])
+
+        hgrp = [None] * T
+
+        def project(f, w):
+            if hgrp[f] is None:
+                hgrp[f] = stage.tile([P, 2, P, 4], BF16, tag="hgrp", name="hgrp", align_bytes=64)
+            acc = mm_pool.tile([P, 4, P], F32, tag="mm", name="acc")
+            for t in range(4):
+                for g in range(2):
+                    cols = slice(128 * g, 128 * g + 128)
+                    nc.tensor.matmul_mx(
+                        out=acc[:, t, :],
+                        lhsT=wq[w][t][:, cols].bitcast(FP8X4),
+                        lhsT_scale=ws[w][t][:, cols],
+                        rhs=xq[f][:, cols].bitcast(FP8X4),
+                        rhs_scale=xs[f][:, cols],
+                        start=(g == 0),
+                        stop=(g == 1),
+                    )
+            nc.scalar.copy(out=hgrp[f][:, w, :, :], in_=acc[:].rearrange("p t r -> p r t"))
+
+        def quantise_h(f):
+            nc.vector.quantize_mx(
+                out=hq[f][:].bitcast(FP8X4),
+                scales=hs[f][:],
+                in_=hgrp[f][:].rearrange("p w r t -> p (w r t)"),
+            )
+
+        def regroup(f):
+            nc.vector.tensor_copy(
+                out=tq_v[:, :, :, f, :],
+                in_=hq[f][:].bitcast(I32).rearrange("p (w g j) -> p g w j", w=2, g=8),
+            )
+            nc.vector.tensor_copy(
+                out=ts_v[:, :, :, f, :],
+                in_=hs[f][:].bitcast(I32).rearrange("p (w g j) -> p g w j", w=2, g=8),
+            )
+
+        sw_acc = [None, None]
+
+        def spatial(f):
+            h = f // 4
+            if sw_acc[h] is None:
+                sw_acc[h] = sw_pool.tile([P, 4, P], F32, tag="sw", name="swacc")
+            nc.tensor.matmul_mx(
+                out=sw_acc[h][:, f % 4, :],
+                lhsT=hq[f][:, 0:128].bitcast(FP8X4),
+                lhsT_scale=hs[f][:, 0:128],
+                rhs=hq[f][:, 128:256].bitcast(FP8X4),
+                rhs_scale=hs[f][:, 128:256],
+                start=True,
+                stop=True,
+            )
+            if f % 4 == 3:
+                sw_sb = stage.tile([P, 4, P], F32, tag="sw_sb", name="sw_sb")
+                nc.scalar.mul(out=sw_sb[:], in_=sw_acc[h][:], mul=1.0 / N)
+                nc.sync.dma_start(
+                    out=out_0[0, 4 * h : 4 * h + 4].rearrange("t j k -> j t k"), in_=sw_sb[:]
+                )
+
+        for t in range(4):
+            transposed(w_raw[0][t], wq[0][t], ws[0][t], W_EXIT[t])
+        for f in (0, 1):
+            transposed(x_raw[f], xq[f], xs[f], X_EXIT[f])
+        project(0, 0)
+        project(1, 0)
+        for t in range(4):
+            transposed(w_raw[1][t], wq[1][t], ws[1][t], W_EXIT[t])
+        for f in (2, 3):
+            transposed(x_raw[f], xq[f], xs[f], X_EXIT[f])
+        project(0, 1)
+        quantise_h(0)
+        project(1, 1)
+        quantise_h(1)
+        for f in (2, 3):
+            project(f, 0)
+            project(f, 1)
+            quantise_h(f)
+        for f in (0, 1):
+            spatial(f)
+            regroup(f)
+        for f in (4, 5, 6, 7):
+            transposed(x_raw[f], xq[f], xs[f], X_EXIT[f])
+        for f in (4, 5):
+            project(f, 0)
+            project(f, 1)
+            quantise_h(f)
+        for f in (2, 3):
+            spatial(f)
+            regroup(f)
+        for f in (6, 7):
+            project(f, 0)
+            project(f, 1)
+            quantise_h(f)
+        for f in (4, 5, 6, 7):
+            spatial(f)
+            regroup(f)
+
+        res = keep.tile([P, 64], F32, name="res")
+        for h in range(2):
+            tw_acc = tp_pool.tile([P, 4, P], F32, tag="tp", name="twacc")
+            for gg in range(4):
+                c0 = 256 * (4 * h + gg)
+                nc.tensor.matmul_mx(
+                    out=tw_acc[:, gg, :],
+                    lhsT=tq[:, c0 : c0 + 128].bitcast(FP8X4),
+                    lhsT_scale=ts[:, c0 : c0 + 128],
+                    rhs=tq[:, c0 + 128 : c0 + 256].bitcast(FP8X4),
+                    rhs_scale=ts[:, c0 + 128 : c0 + 256],
+                    start=True,
+                    stop=True,
+                )
+            prod = stage.tile([P, 32, 16], F32, tag="prod", name="prod")
+            nc.vector.tensor_tensor(
+                out=prod[:],
+                in0=tw_acc[:].rearrange("p g (s j) -> p (g s) j", j=16),
+                in1=m16[:].unsqueeze(1).to_broadcast([P, 32, 16]),
+                op=ALU.mult,
+            )
+            nc.vector.tensor_reduce(out=res[:, 32 * h : 32 * h + 32], in_=prod[:], axis=AX.X, op=ALU.add)
+        for t in range(T):
+            nc.sync.dma_start(
+                out=out_1[0, t].rearrange("(g j) s -> j g s", j=16),
+                in_=res[16 * t : 16 * t + 16, :].rearrange("p (g s) -> p g s", s=8),
+            )

@@ -18,17 +18,131 @@ N = 128
 D = 1024
 L = 512
 FLOPS = 2 * (T * N) * D * (2 * L) + 2 * T * N * N * L + 2 * N * T * T * L
-
-W_EXIT = ("s", "v", "s", "v")
-X_EXIT = ("s", "v", "s", "v", "s", "s", "s", "s")
+LOADS = ("wt0", "wt1", "wt2", "wt3", "x0", "x1", "x2", "wp0", "wp1", "wp2", "wp3", "x3", "x4", "x5", "x6", "x7")
+STEPS = (
+    ("Tpe", "wt0"),
+    ("Tex", "wt0", "s"),
+    ("Tpe", "wt1"),
+    ("Tex", "wt1", "s"),
+    ("Tq", "wt0"),
+    ("Tpe", "wt2"),
+    ("Tex", "wt2", "s"),
+    ("Tq", "wt1"),
+    ("Tpe", "wt3"),
+    ("Tex", "wt3", "s"),
+    ("Tq", "wt2"),
+    ("Tpe", "x0"),
+    ("Tex", "x0", "s"),
+    ("Tq", "wt3"),
+    ("Tpe", "x1"),
+    ("Tex", "x1", "s"),
+    ("Tq", "x0"),
+    ("Tpe", "x2"),
+    ("Tex", "x2", "s"),
+    ("Tq", "x1"),
+    ("Mpe", 0, 0),
+    ("Tq", "x2"),
+    ("Mpe", 1, 0),
+    ("Mex", 0, 0, "s"),
+    ("Tpe", "wp0"),
+    ("Mex", 1, 0, "s"),
+    ("Tpe", "wp1"),
+    ("Tex", "wp0", "v"),
+    ("Tpe", "wp2"),
+    ("Tex", "wp1", "s"),
+    ("Tq", "wp0"),
+    ("Tpe", "wp3"),
+    ("Tex", "wp2", "s"),
+    ("Tq", "wp1"),
+    ("Mpe", 2, 0),
+    ("Tex", "wp3", "v"),
+    ("Tpe", "x3"),
+    ("Mex", 2, 0, "s"),
+    ("Tq", "wp2"),
+    ("Tq", "wp3"),
+    ("Tpe", "x4"),
+    ("Tex", "x3", "s"),
+    ("Tex", "x4", "v"),
+    ("Mpe", 0, 1),
+    ("Tq", "x3"),
+    ("Mpe", 1, 1),
+    ("Tq", "x4"),
+    ("Mex", 0, 1, "s"),
+    ("Mpe", 2, 1),
+    ("Mex", 1, 1, "s"),
+    ("Hq", 0),
+    ("Mv", 0),
+    ("Mpe", 3, 0),
+    ("Mex", 2, 1, "s"),
+    ("Hq", 1),
+    ("Mv", 1),
+    ("Mpe", 3, 1),
+    ("Mex", 3, 0, "s"),
+    ("Hq", 2),
+    ("Mv", 2),
+    ("SWpe", 0),
+    ("SWpe", 1),
+    ("Mex", 3, 1, "s"),
+    ("Tpe", "x5"),
+    ("Tpe", "x6"),
+    ("Tex", "x5", "s"),
+    ("Hq", 3),
+    ("Tpe", "x7"),
+    ("Tex", "x6", "v"),
+    ("Mpe", 4, 0),
+    ("Tex", "x7", "s"),
+    ("Tq", "x5"),
+    ("Mpe", 4, 1),
+    ("Tq", "x6"),
+    ("Mex", 4, 0, "s"),
+    ("Tq", "x7"),
+    ("SWpe", 2),
+    ("Mv", 3),
+    ("SWpe", 3),
+    ("Mex", 4, 1, "s"),
+    ("Mpe", 5, 0),
+    ("SWex", 0, "v"),
+    ("Mpe", 5, 1),
+    ("Mex", 5, 0, "s"),
+    ("Hq", 4),
+    ("Mv", 4),
+    ("Mex", 5, 1, "s"),
+    ("SWpe", 4),
+    ("Mpe", 6, 0),
+    ("Hq", 5),
+    ("Mpe", 6, 1),
+    ("Mex", 6, 0, "s"),
+    ("Mv", 5),
+    ("SWpe", 5),
+    ("Mpe", 7, 0),
+    ("Mex", 6, 1, "s"),
+    ("Mpe", 7, 1),
+    ("Hq", 6),
+    ("Mex", 7, 0, "s"),
+    ("Mv", 6),
+    ("Hq", 7, 0),
+    ("Mv", 7, 0),
+    ("Mex", 7, 1, "s"),
+    ("SWpe", 6),
+    ("Hq", 7, 1),
+    ("Mv", 7, 1),
+    ("TWpe", 0),
+    ("TWpe", 1),
+    ("SWpe", 7),
+    ("TWmul", 0),
+    ("SWex", 1, "s"),
+    ("TWmul", 1),
+    ("TWred",),
+)
 
 
 def tile_higcin_volleyball_pa_kernel(tc, x, Wtheta, Wphi, out_0, out_1):
     nc = tc.nc
     with ExitStack() as ctx:
+        ctx.enter_context(tc.manual_schedule())
         raw = ctx.enter_context(tc.tile_pool(name="raw", bufs=1))
         keep = ctx.enter_context(tc.tile_pool(name="keep", bufs=1))
-        stage = ctx.enter_context(tc.tile_pool(name="stage", bufs=4))
+        stage = ctx.enter_context(tc.tile_pool(name="stage", bufs=6))
         tp_pool = ctx.enter_context(tc.psum_pool(name="tp", bufs=3))
         mm_pool = ctx.enter_context(tc.psum_pool(name="mm", bufs=4))
         sw_pool = ctx.enter_context(tc.psum_pool(name="swp", bufs=1))
@@ -37,103 +151,127 @@ def tile_higcin_volleyball_pa_kernel(tc, x, Wtheta, Wphi, out_0, out_1):
             Wtheta.rearrange("(p t) d -> p t d", t=4),
             Wphi.rearrange("(p t) d -> p t d", t=4),
         )
-        w_raw = [[raw.tile([P, D], BF16, name="wraw%d_%d" % (w, t)) for t in range(4)] for w in range(2)]
-        x_raw = [raw.tile([P, D], BF16, name="xraw%d" % f) for f in range(T)]
-
-        def load_w(w):
-            for t in range(4):
-                nc.sync.dma_start(out=w_raw[w][t][:], in_=w_dram[w][:, t, :])
-
-        def load_x(f):
-            nc.sync.dma_start(out=x_raw[f][:], in_=x[0, f])
-
-        load_w(0)
-        load_x(0)
-        load_x(1)
-        load_w(1)
-        for f in range(2, T):
-            load_x(f)
+        src = {}
+        codes = {}
+        planes = {}
+        for u in LOADS:
+            src[u] = raw.tile([P, D], BF16, name="raw_" + u)
+            codes[u] = keep.tile([P, 256], U32, name="q_" + u, align_bytes=64)
+            planes[u] = keep.tile([P, 256], U8, name="s_" + u, align_bytes=64)
+            k = int(u[-1])
+            if u[0] == "x":
+                nc.sync.dma_start(out=src[u][:], in_=x[0, k])
+            else:
+                nc.sync.dma_start(out=src[u][:], in_=w_dram[0 if u[1] == "t" else 1][:, k, :])
 
         ident = keep.tile([P, P], F32, name="ident")
         make_identity(nc, ident[:])
+        hq = [keep.tile([P, 256], U32, name="hq%d" % f, align_bytes=64) for f in range(T)]
+        hs = [keep.tile([P, 256], U8, name="hs%d" % f, align_bytes=64) for f in range(T)]
+        for f in range(T):
+            nc.vector.memset(hs[f][:].bitcast(I32), 0)
         m16raw = keep.tile([P, 16], F32, name="m16raw")
         nc.vector.tensor_reduce(
             out=m16raw[:], in_=ident[:].rearrange("p (t j) -> p j t", j=16), axis=AX.X, op=ALU.add
         )
         m16 = keep.tile([P, 16], F32, name="m16")
         nc.vector.tensor_scalar_mul(out=m16[:], in0=m16raw[:], scalar1=1.0 / T)
-
-        wq = [[keep.tile([P, 256], U32, name="wq%d_%d" % (w, t), align_bytes=64) for t in range(4)] for w in range(2)]
-        ws = [[keep.tile([P, 256], U8, name="ws%d_%d" % (w, t), align_bytes=64) for t in range(4)] for w in range(2)]
-        xq = [keep.tile([P, 256], U32, name="xq%d" % f, align_bytes=64) for f in range(T)]
-        xs = [keep.tile([P, 256], U8, name="xs%d" % f, align_bytes=64) for f in range(T)]
-        hq = [keep.tile([P, 256], U32, name="hq%d" % f, align_bytes=64) for f in range(T)]
-        hs = [keep.tile([P, 256], U8, name="hs%d" % f, align_bytes=64) for f in range(T)]
-        for f in range(T):
-            nc.vector.memset(hs[f][:].bitcast(I32), 0)
         tq = keep.tile([P, 2048], U32, name="tq", align_bytes=64)
         ts = keep.tile([P, 2048], U8, name="ts", align_bytes=64)
         tq_v = tq[:].bitcast(I32).rearrange("p (g w t j) -> p g w t j", g=8, w=2, t=T)
         ts_v = ts[:].bitcast(I32).rearrange("p (g w t j) -> p g w t j", g=8, w=2, t=T)
+        res = keep.tile([P, 64], F32, name="res")
+        prod = keep.tile([P, 64, 16], F32, name="prod")
 
-        def transposed(src, codes, scales, eng):
-            bank = tp_pool.tile([P, 2, 2, P], F32, tag="tp", name="bank")
-            words = src[:].bitcast(F32)
-            for g in range(2):
-                for u in range(2):
-                    c0 = 256 * g + 128 * u
-                    nc.tensor.transpose(bank[:, g, u, :], words[:, c0 : c0 + 128], ident[:])
-            grouped = stage.tile([P, 4 * 256], BF16, tag="grouped", name="grouped", align_bytes=64)
-            dst = grouped[:].bitcast(F32).rearrange("p (g r u) -> p g r u", g=2, u=2)
-            srcv = bank[:].rearrange("p g u r -> p g r u")
+        banks = {}
+        grouped = {}
+        accs = {}
+        hgrp = {}
+        sw_acc = {}
+        tw_acc = {}
+
+        def copy_out(eng, out, in_):
             if eng == "s":
-                nc.scalar.copy(out=dst, in_=srcv)
+                nc.scalar.copy(out=out, in_=in_)
             else:
-                nc.vector.tensor_copy(out=dst, in_=srcv)
-            nc.vector.quantize_mx(out=codes[:].bitcast(FP8X4), scales=scales[:], in_=grouped[:])
+                nc.vector.tensor_copy(out=out, in_=in_)
 
-        hgrp = [None] * T
+        def Tpe(u):
+            banks[u] = tp_pool.tile([P, 2, 2, P], F32, tag="tp", name="bank")
+            words = src[u][:].bitcast(F32)
+            for g in range(2):
+                for h in range(2):
+                    c0 = 256 * g + 128 * h
+                    nc.tensor.transpose(banks[u][:, g, h, :], words[:, c0 : c0 + 128], ident[:])
 
-        def project(f, w):
-            if hgrp[f] is None:
-                hgrp[f] = stage.tile([P, 2, P, 4], BF16, tag="hgrp", name="hgrp", align_bytes=64)
-            acc = mm_pool.tile([P, 4, P], F32, tag="mm", name="acc")
-            for t in range(4):
+        def Tex(u, eng):
+            grouped[u] = stage.tile([P, 1024], BF16, tag="grouped", name="grouped", align_bytes=64)
+            copy_out(
+                eng,
+                grouped[u][:].bitcast(F32).rearrange("p (g r h) -> p g r h", g=2, h=2),
+                banks[u][:].rearrange("p g h r -> p g r h"),
+            )
+
+        def Tq(u):
+            nc.vector.quantize_mx(out=codes[u][:].bitcast(FP8X4), scales=planes[u][:], in_=grouped[u][:])
+
+        def Mpe(f, w, tiles=(0, 1, 2, 3)):
+            if (f, w) not in accs:
+                accs[(f, w)] = mm_pool.tile([P, 4, P], F32, tag="mm", name="acc")
+            xu = "x%d" % f
+            for t in tiles:
+                wu = ("wt%d" if w == 0 else "wp%d") % t
                 for g in range(2):
                     cols = slice(128 * g, 128 * g + 128)
                     nc.tensor.matmul_mx(
-                        out=acc[:, t, :],
-                        lhsT=wq[w][t][:, cols].bitcast(FP8X4),
-                        lhsT_scale=ws[w][t][:, cols],
-                        rhs=xq[f][:, cols].bitcast(FP8X4),
-                        rhs_scale=xs[f][:, cols],
+                        out=accs[(f, w)][:, t, :],
+                        lhsT=codes[wu][:, cols].bitcast(FP8X4),
+                        lhsT_scale=planes[wu][:, cols],
+                        rhs=codes[xu][:, cols].bitcast(FP8X4),
+                        rhs_scale=planes[xu][:, cols],
                         start=(g == 0),
                         stop=(g == 1),
                     )
-            nc.scalar.copy(out=hgrp[f][:, w, :, :], in_=acc[:].rearrange("p t r -> p r t"))
 
-        def quantise_h(f):
-            nc.vector.quantize_mx(
-                out=hq[f][:].bitcast(FP8X4),
-                scales=hs[f][:],
-                in_=hgrp[f][:].rearrange("p w r t -> p (w r t)"),
-            )
+        def Mex(f, w, eng):
+            if f not in hgrp:
+                hgrp[f] = stage.tile([P, 2, P, 4], BF16, tag="hgrp", name="hgrp", align_bytes=64)
+            copy_out(eng, hgrp[f][:, w, :, :], accs[(f, w)][:].rearrange("p t r -> p r t"))
 
-        def regroup(f):
-            nc.vector.tensor_copy(
-                out=tq_v[:, :, :, f, :],
-                in_=hq[f][:].bitcast(I32).rearrange("p (w g j) -> p g w j", w=2, g=8),
-            )
-            nc.vector.tensor_copy(
-                out=ts_v[:, :, :, f, :],
-                in_=hs[f][:].bitcast(I32).rearrange("p (w g j) -> p g w j", w=2, g=8),
-            )
+        def Hq(f, w=None):
+            if w is None:
+                nc.vector.quantize_mx(
+                    out=hq[f][:].bitcast(FP8X4), scales=hs[f][:], in_=hgrp[f][:].rearrange("p w r t -> p (w r t)")
+                )
+            else:
+                cols = slice(128 * w, 128 * w + 128)
+                nc.vector.quantize_mx(
+                    out=hq[f][:, cols].bitcast(FP8X4),
+                    scales=hs[f][:, cols],
+                    in_=hgrp[f][:, w, :, :].rearrange("p r t -> p (r t)"),
+                )
 
-        sw_acc = [None, None]
+        def Mv(f, w=None):
+            if w is None:
+                nc.vector.tensor_copy(
+                    out=tq_v[:, :, :, f, :], in_=hq[f][:].bitcast(I32).rearrange("p (w g j) -> p g w j", w=2, g=8)
+                )
+                nc.vector.tensor_copy(
+                    out=ts_v[:, :, :, f, :], in_=hs[f][:].bitcast(I32).rearrange("p (w g j) -> p g w j", w=2, g=8)
+                )
+            else:
+                nc.vector.tensor_copy(
+                    out=tq_v[:, :, w, f, :],
+                    in_=hq[f][:].bitcast(I32)[:, 128 * w : 128 * w + 128].rearrange("p (g j) -> p g j", g=8),
+                )
+                nc.vector.tensor_copy(
+                    out=ts_v[:, :, w, f, :],
+                    in_=hs[f][:].bitcast(I32)[:, 32 * w : 32 * w + 32].rearrange("p (g j) -> p g j", g=8),
+                )
 
-        def spatial(f):
+        def SWpe(f):
             h = f // 4
-            if sw_acc[h] is None:
+            if h not in sw_acc:
                 sw_acc[h] = sw_pool.tile([P, 4, P], F32, tag="sw", name="swacc")
             nc.tensor.matmul_mx(
                 out=sw_acc[h][:, f % 4, :],
@@ -144,58 +282,21 @@ def tile_higcin_volleyball_pa_kernel(tc, x, Wtheta, Wphi, out_0, out_1):
                 start=True,
                 stop=True,
             )
-            if f % 4 == 3:
-                sw_sb = stage.tile([P, 4, P], F32, tag="sw_sb", name="sw_sb")
+
+        def SWex(h, eng):
+            sw_sb = stage.tile([P, 4, P], F32, tag="sw_sb", name="sw_sb")
+            if eng == "s":
                 nc.scalar.mul(out=sw_sb[:], in_=sw_acc[h][:], mul=1.0 / N)
-                nc.sync.dma_start(
-                    out=out_0[0, 4 * h : 4 * h + 4].rearrange("t j k -> j t k"), in_=sw_sb[:]
-                )
+            else:
+                nc.vector.tensor_scalar_mul(out=sw_sb[:], in0=sw_acc[h][:], scalar1=1.0 / N)
+            nc.sync.dma_start(out=out_0[0, 4 * h : 4 * h + 4].rearrange("t j k -> j t k"), in_=sw_sb[:])
 
-        for t in range(4):
-            transposed(w_raw[0][t], wq[0][t], ws[0][t], W_EXIT[t])
-        for f in (0, 1):
-            transposed(x_raw[f], xq[f], xs[f], X_EXIT[f])
-        project(0, 0)
-        project(1, 0)
-        for t in range(4):
-            transposed(w_raw[1][t], wq[1][t], ws[1][t], W_EXIT[t])
-        for f in (2, 3):
-            transposed(x_raw[f], xq[f], xs[f], X_EXIT[f])
-        project(0, 1)
-        quantise_h(0)
-        project(1, 1)
-        quantise_h(1)
-        for f in (2, 3):
-            project(f, 0)
-            project(f, 1)
-            quantise_h(f)
-        for f in (0, 1):
-            spatial(f)
-            regroup(f)
-        for f in (4, 5, 6, 7):
-            transposed(x_raw[f], xq[f], xs[f], X_EXIT[f])
-        for f in (4, 5):
-            project(f, 0)
-            project(f, 1)
-            quantise_h(f)
-        for f in (2, 3):
-            spatial(f)
-            regroup(f)
-        for f in (6, 7):
-            project(f, 0)
-            project(f, 1)
-            quantise_h(f)
-        for f in (4, 5, 6, 7):
-            spatial(f)
-            regroup(f)
-
-        res = keep.tile([P, 64], F32, name="res")
-        for h in range(2):
-            tw_acc = tp_pool.tile([P, 4, P], F32, tag="tp", name="twacc")
+        def TWpe(h):
+            tw_acc[h] = tp_pool.tile([P, 4, P], F32, tag="tp", name="twacc")
             for gg in range(4):
                 c0 = 256 * (4 * h + gg)
                 nc.tensor.matmul_mx(
-                    out=tw_acc[:, gg, :],
+                    out=tw_acc[h][:, gg, :],
                     lhsT=tq[:, c0 : c0 + 128].bitcast(FP8X4),
                     lhsT_scale=ts[:, c0 : c0 + 128],
                     rhs=tq[:, c0 + 128 : c0 + 256].bitcast(FP8X4),
@@ -203,16 +304,27 @@ def tile_higcin_volleyball_pa_kernel(tc, x, Wtheta, Wphi, out_0, out_1):
                     start=True,
                     stop=True,
                 )
-            prod = stage.tile([P, 32, 16], F32, tag="prod", name="prod")
+
+        def TWmul(h):
             nc.vector.tensor_tensor(
-                out=prod[:],
-                in0=tw_acc[:].rearrange("p g (s j) -> p (g s) j", j=16),
+                out=prod[:, 32 * h : 32 * h + 32, :],
+                in0=tw_acc[h][:].rearrange("p g (s j) -> p (g s) j", j=16),
                 in1=m16[:].unsqueeze(1).to_broadcast([P, 32, 16]),
                 op=ALU.mult,
             )
-            nc.vector.tensor_reduce(out=res[:, 32 * h : 32 * h + 32], in_=prod[:], axis=AX.X, op=ALU.add)
-        for t in range(T):
-            nc.sync.dma_start(
-                out=out_1[0, t].rearrange("(g j) s -> j g s", j=16),
-                in_=res[16 * t : 16 * t + 16, :].rearrange("p (g s) -> p g s", s=8),
-            )
+
+        def TWred():
+            nc.vector.tensor_reduce(out=res[:], in_=prod[:], axis=AX.X, op=ALU.add)
+            for t in range(T):
+                q = nc.sync if t % 2 == 0 else nc.scalar
+                q.dma_start(
+                    out=out_1[0, t].rearrange("(g j) s -> j g s", j=16),
+                    in_=res[16 * t : 16 * t + 16, :].rearrange("p (g s) -> p g s", s=8),
+                )
+
+        table = {
+            "Tpe": Tpe, "Tex": Tex, "Tq": Tq, "Mpe": Mpe, "Mex": Mex, "Hq": Hq, "Mv": Mv,
+            "SWpe": SWpe, "SWex": SWex, "TWpe": TWpe, "TWmul": TWmul, "TWred": TWred,
+        }
+        for step in STEPS:
+            table[step[0]](*step[1:])

@@ -62,12 +62,15 @@ STEPS = (
     ("Tq", "wp3"),
     ("Tpe", "x4"),
     ("Tex", "x3", "s"),
+    ("Tpe", "x5"),
     ("Tex", "x4", "v"),
     ("Mpe", 0, 1),
+    ("Tex", "x5", "s"),
     ("Tq", "x3"),
-    ("Mpe", 1, 1),
     ("Tq", "x4"),
+    ("Mpe", 1, 1),
     ("Mex", 0, 1, "s"),
+    ("Tq", "x5"),
     ("Mpe", 2, 1),
     ("Mex", 1, 1, "s"),
     ("Hq", 0),
@@ -83,15 +86,12 @@ STEPS = (
     ("SWpe", 0),
     ("SWpe", 1),
     ("Mex", 3, 1, "s"),
-    ("Tpe", "x5"),
     ("Tpe", "x6"),
-    ("Tex", "x5", "s"),
-    ("Hq", 3),
     ("Tpe", "x7"),
-    ("Tex", "x6", "v"),
+    ("Tex", "x6", "s"),
+    ("Hq", 3),
     ("Mpe", 4, 0),
-    ("Tex", "x7", "s"),
-    ("Tq", "x5"),
+    ("Tex", "x7", "v"),
     ("Mpe", 4, 1),
     ("Tq", "x6"),
     ("Mex", 4, 0, "s"),
@@ -99,39 +99,39 @@ STEPS = (
     ("SWpe", 2),
     ("Mv", 3),
     ("SWpe", 3),
-    ("Mex", 4, 1, "s"),
     ("Mpe", 5, 0),
-    ("SWex", 0, "v"),
+    ("SWex", 0, "s"),
+    ("Mex", 4, 1, "v"),
     ("Mpe", 5, 1),
     ("Mex", 5, 0, "s"),
     ("Hq", 4),
     ("Mv", 4),
-    ("Mex", 5, 1, "s"),
-    ("SWpe", 4),
     ("Mpe", 6, 0),
-    ("Hq", 5),
+    ("Mex", 5, 1, "s"),
     ("Mpe", 6, 1),
     ("Mex", 6, 0, "s"),
+    ("Hq", 5),
     ("Mv", 5),
-    ("SWpe", 5),
     ("Mpe", 7, 0),
-    ("Mex", 6, 1, "s"),
+    ("Mex", 6, 1, "v"),
     ("Mpe", 7, 1),
-    ("Hq", 6),
     ("Mex", 7, 0, "s"),
+    ("Hq", 6),
     ("Mv", 6),
+    ("Mex", 7, 1, "s"),
     ("Hq", 7, 0),
     ("Mv", 7, 0),
-    ("Mex", 7, 1, "s"),
-    ("SWpe", 6),
     ("Hq", 7, 1),
     ("Mv", 7, 1),
     ("TWpe", 0),
     ("TWpe", 1),
-    ("SWpe", 7),
     ("TWmul", 0),
-    ("SWex", 1, "s"),
+    ("SWpe", 4),
+    ("SWpe", 5),
+    ("SWpe", 6),
+    ("SWpe", 7),
     ("TWmul", 1),
+    ("SWex", 1, "s"),
     ("TWred",),
 )
 

@@ -20,24 +20,32 @@ L = 512
 FLOPS = 2 * (T * N) * D * (2 * L) + 2 * T * N * N * L + 2 * N * T * T * L
 LOADS = ("wt0", "wt1", "wt2", "wt3", "x0", "x1", "x2", "wp0", "wp1", "wp2", "wp3", "x3", "x4", "x5", "x6", "x7")
 STEPS = (
+    ("Dm", 512, 5),
     ("Tpe", "wt0"),
+    ("Dm", 512),
     ("Tex", "wt0", "s"),
     ("Tpe", "wt1"),
+    ("Dm", 512),
     ("Tex", "wt1", "s"),
     ("Tq", "wt0"),
     ("Tpe", "wt2"),
+    ("Dm", 512),
     ("Tex", "wt2", "s"),
     ("Tq", "wt1"),
     ("Tpe", "wt3"),
+    ("Dm", 512),
     ("Tex", "wt3", "s"),
     ("Tq", "wt2"),
     ("Tpe", "x0"),
+    ("Dm", 512),
     ("Tex", "x0", "s"),
     ("Tq", "wt3"),
     ("Tpe", "x1"),
+    ("Dm", 512),
     ("Tex", "x1", "s"),
     ("Tq", "x0"),
     ("Tpe", "x2"),
+    ("Dm", 512),
     ("Tex", "x2", "s"),
     ("Tq", "x1"),
     ("Mpe", 0, 0),
@@ -62,15 +70,12 @@ STEPS = (
     ("Tq", "wp3"),
     ("Tpe", "x4"),
     ("Tex", "x3", "s"),
-    ("Tpe", "x5"),
     ("Tex", "x4", "v"),
     ("Mpe", 0, 1),
-    ("Tex", "x5", "s"),
     ("Tq", "x3"),
-    ("Tq", "x4"),
     ("Mpe", 1, 1),
+    ("Tq", "x4"),
     ("Mex", 0, 1, "s"),
-    ("Tq", "x5"),
     ("Mpe", 2, 1),
     ("Mex", 1, 1, "s"),
     ("Hq", 0),
@@ -86,12 +91,15 @@ STEPS = (
     ("SWpe", 0),
     ("SWpe", 1),
     ("Mex", 3, 1, "s"),
+    ("Tpe", "x5"),
     ("Tpe", "x6"),
-    ("Tpe", "x7"),
-    ("Tex", "x6", "s"),
+    ("Tex", "x5", "s"),
     ("Hq", 3),
+    ("Tpe", "x7"),
+    ("Tex", "x6", "v"),
     ("Mpe", 4, 0),
-    ("Tex", "x7", "v"),
+    ("Tex", "x7", "s"),
+    ("Tq", "x5"),
     ("Mpe", 4, 1),
     ("Tq", "x6"),
     ("Mex", 4, 0, "s"),
@@ -99,39 +107,39 @@ STEPS = (
     ("SWpe", 2),
     ("Mv", 3),
     ("SWpe", 3),
+    ("Mex", 4, 1, "s"),
     ("Mpe", 5, 0),
-    ("SWex", 0, "s"),
-    ("Mex", 4, 1, "v"),
+    ("SWex", 0, "v"),
     ("Mpe", 5, 1),
     ("Mex", 5, 0, "s"),
     ("Hq", 4),
     ("Mv", 4),
-    ("Mpe", 6, 0),
     ("Mex", 5, 1, "s"),
+    ("SWpe", 4),
+    ("Mpe", 6, 0),
+    ("Hq", 5),
     ("Mpe", 6, 1),
     ("Mex", 6, 0, "s"),
-    ("Hq", 5),
     ("Mv", 5),
+    ("SWpe", 5),
     ("Mpe", 7, 0),
-    ("Mex", 6, 1, "v"),
+    ("Mex", 6, 1, "s"),
     ("Mpe", 7, 1),
-    ("Mex", 7, 0, "s"),
     ("Hq", 6),
+    ("Mex", 7, 0, "s"),
     ("Mv", 6),
-    ("Mex", 7, 1, "s"),
     ("Hq", 7, 0),
     ("Mv", 7, 0),
+    ("Mex", 7, 1, "s"),
+    ("SWpe", 6),
     ("Hq", 7, 1),
     ("Mv", 7, 1),
     ("TWpe", 0),
     ("TWpe", 1),
-    ("TWmul", 0),
-    ("SWpe", 4),
-    ("SWpe", 5),
-    ("SWpe", 6),
     ("SWpe", 7),
-    ("TWmul", 1),
+    ("TWmul", 0),
     ("SWex", 1, "s"),
+    ("TWmul", 1),
     ("TWred",),
 )
 
@@ -164,6 +172,8 @@ def tile_higcin_volleyball_pa_kernel(tc, x, Wtheta, Wphi, out_0, out_1):
             else:
                 nc.sync.dma_start(out=src[u][:], in_=w_dram[0 if u[1] == "t" else 1][:, k, :])
 
+        zb = keep.tile([P, 512], BF16, name="zb")
+        nc.vector.memset(zb[:], 0.0)
         ident = keep.tile([P, P], F32, name="ident")
         make_identity(nc, ident[:])
         hq = [keep.tile([P, 256], U32, name="hq%d" % f, align_bytes=64) for f in range(T)]
@@ -182,6 +192,12 @@ def tile_higcin_volleyball_pa_kernel(tc, x, Wtheta, Wphi, out_0, out_1):
         ts_v = ts[:].bitcast(I32).rearrange("p (g w t j) -> p g w t j", g=8, w=2, t=T)
         res = keep.tile([P, 64], F32, name="res")
         prod = keep.tile([P, 64, 16], F32, name="prod")
+
+        warm = sw_pool.tile([P, 512], F32, tag="sw", name="warm")
+
+        def Dm(cols, n=1):
+            for i in range(n):
+                nc.tensor.matmul(out=warm[:, 0:cols], lhsT=zb[:, 0:128], rhs=zb[:, 0:cols], start=True, stop=True)
 
         banks = {}
         grouped = {}
@@ -324,7 +340,7 @@ def tile_higcin_volleyball_pa_kernel(tc, x, Wtheta, Wphi, out_0, out_1):
 
         table = {
             "Tpe": Tpe, "Tex": Tex, "Tq": Tq, "Mpe": Mpe, "Mex": Mex, "Hq": Hq, "Mv": Mv,
-            "SWpe": SWpe, "SWex": SWex, "TWpe": TWpe, "TWmul": TWmul, "TWred": TWred,
+            "SWpe": SWpe, "Dm": Dm, "SWex": SWex, "TWpe": TWpe, "TWmul": TWmul, "TWred": TWred,
         }
         for step in STEPS:
             table[step[0]](*step[1:])

@@ -70,12 +70,15 @@ STEPS = (
     ("Tq", "wp3"),
     ("Tpe", "x4"),
     ("Tex", "x3", "s"),
+    ("Tpe", "x5"),
     ("Tex", "x4", "v"),
     ("Mpe", 0, 1),
+    ("Tex", "x5", "s"),
     ("Tq", "x3"),
-    ("Mpe", 1, 1),
     ("Tq", "x4"),
+    ("Mpe", 1, 1),
     ("Mex", 0, 1, "s"),
+    ("Tq", "x5"),
     ("Mpe", 2, 1),
     ("Mex", 1, 1, "s"),
     ("Hq", 0),
@@ -91,15 +94,12 @@ STEPS = (
     ("SWpe", 0),
     ("SWpe", 1),
     ("Mex", 3, 1, "s"),
-    ("Tpe", "x5"),
     ("Tpe", "x6"),
-    ("Tex", "x5", "s"),
-    ("Hq", 3),
     ("Tpe", "x7"),
-    ("Tex", "x6", "v"),
+    ("Tex", "x6", "s"),
+    ("Hq", 3),
     ("Mpe", 4, 0),
-    ("Tex", "x7", "s"),
-    ("Tq", "x5"),
+    ("Tex", "x7", "v"),
     ("Mpe", 4, 1),
     ("Tq", "x6"),
     ("Mex", 4, 0, "s"),
@@ -114,32 +114,32 @@ STEPS = (
     ("Mex", 5, 0, "s"),
     ("Hq", 4),
     ("Mv", 4),
-    ("Mex", 5, 1, "s"),
-    ("SWpe", 4),
     ("Mpe", 6, 0),
-    ("Hq", 5),
+    ("Mex", 5, 1, "s"),
     ("Mpe", 6, 1),
     ("Mex", 6, 0, "s"),
+    ("Hq", 5),
     ("Mv", 5),
-    ("SWpe", 5),
     ("Mpe", 7, 0),
     ("Mex", 6, 1, "s"),
     ("Mpe", 7, 1),
-    ("Hq", 6),
     ("Mex", 7, 0, "s"),
+    ("Hq", 6),
     ("Mv", 6),
+    ("Mex", 7, 1, "s"),
     ("Hq", 7, 0),
     ("Mv", 7, 0),
-    ("Mex", 7, 1, "s"),
-    ("SWpe", 6),
     ("Hq", 7, 1),
     ("Mv", 7, 1),
     ("TWpe", 0),
     ("TWpe", 1),
-    ("SWpe", 7),
     ("TWmul", 0),
-    ("SWex", 1, "s"),
+    ("SWpe", 4),
+    ("SWpe", 5),
+    ("SWpe", 6),
+    ("SWpe", 7),
     ("TWmul", 1),
+    ("SWex", 1, "s"),
     ("TWred",),
 )
 
@@ -174,6 +174,8 @@ def tile_higcin_volleyball_pa_kernel(tc, x, Wtheta, Wphi, out_0, out_1):
 
         zb = keep.tile([P, 512], BF16, name="zb")
         nc.vector.memset(zb[:], 0.0)
+        scr = keep.tile([P, 1], F32, name="scr")
+        nc.scalar.mul(out=scr[:], in_=zb[:, 0:1], mul=1.0)
         ident = keep.tile([P, P], F32, name="ident")
         make_identity(nc, ident[:])
         hq = [keep.tile([P, 256], U32, name="hq%d" % f, align_bytes=64) for f in range(T)]

@@ -13,135 +13,20 @@ ALU = mybir.AluOpType
 AX = mybir.AxisListType
 
 P = 128
-T = 8
-N = 128
-D = 1024
-L = 512
-FLOPS = 2 * (T * N) * D * (2 * L) + 2 * T * N * N * L + 2 * N * T * T * L
-LOADS = ("wt0", "wt1", "wt2", "wt3", "x0", "x1", "x2", "wp0", "wp1", "wp2", "wp3", "x3", "x4", "x5", "x6", "x7")
-STEPS = (
-    ("Dm", 512, 5),
-    ("Tpe", "wt0"),
-    ("Dm", 512),
-    ("Tex", "wt0", "s"),
-    ("Tpe", "wt1"),
-    ("Dm", 512),
-    ("Tex", "wt1", "s"),
-    ("Tq", "wt0"),
-    ("Tpe", "wt2"),
-    ("Dm", 512),
-    ("Tex", "wt2", "s"),
-    ("Tq", "wt1"),
-    ("Tpe", "wt3"),
-    ("Dm", 512),
-    ("Tex", "wt3", "s"),
-    ("Tq", "wt2"),
-    ("Tpe", "x0"),
-    ("Dm", 512),
-    ("Tex", "x0", "s"),
-    ("Tq", "wt3"),
-    ("Tpe", "x1"),
-    ("Dm", 512),
-    ("Tex", "x1", "s"),
-    ("Tq", "x0"),
-    ("Tpe", "x2"),
-    ("Dm", 512),
-    ("Tex", "x2", "s"),
-    ("Tq", "x1"),
-    ("Mpe", 0, 0),
-    ("Tq", "x2"),
-    ("Mpe", 1, 0),
-    ("Mex", 0, 0, "s"),
-    ("Tpe", "wp0"),
-    ("Mex", 1, 0, "s"),
-    ("Tpe", "wp1"),
-    ("Tex", "wp0", "v"),
-    ("Tpe", "wp2"),
-    ("Tex", "wp1", "s"),
-    ("Tq", "wp0"),
-    ("Tpe", "wp3"),
-    ("Tex", "wp2", "s"),
-    ("Tq", "wp1"),
-    ("Mpe", 2, 0),
-    ("Tex", "wp3", "v"),
-    ("Tpe", "x3"),
-    ("Mex", 2, 0, "s"),
-    ("Tq", "wp2"),
-    ("Tq", "wp3"),
-    ("Tpe", "x4"),
-    ("Tex", "x3", "s"),
-    ("Tpe", "x5"),
-    ("Tex", "x4", "v"),
-    ("Mpe", 0, 1),
-    ("Tex", "x5", "s"),
-    ("Tq", "x3"),
-    ("Tq", "x4"),
-    ("Mpe", 1, 1),
-    ("Mex", 0, 1, "s"),
-    ("Tq", "x5"),
-    ("Mpe", 2, 1),
-    ("Mex", 1, 1, "s"),
-    ("Hq", 0),
-    ("Mv", 0),
-    ("Mpe", 3, 0),
-    ("Mex", 2, 1, "s"),
-    ("Hq", 1),
-    ("Mv", 1),
-    ("Mpe", 3, 1),
-    ("Mex", 3, 0, "s"),
-    ("Hq", 2),
-    ("Mv", 2),
-    ("SWpe", 0),
-    ("SWpe", 1),
-    ("Mex", 3, 1, "s"),
-    ("Tpe", "x6"),
-    ("Tpe", "x7"),
-    ("Tex", "x6", "s"),
-    ("Hq", 3),
-    ("Mpe", 4, 0),
-    ("Tex", "x7", "v"),
-    ("Mpe", 4, 1),
-    ("Tq", "x6"),
-    ("Mex", 4, 0, "s"),
-    ("Tq", "x7"),
-    ("SWpe", 2),
-    ("Mv", 3),
-    ("SWpe", 3),
-    ("Mex", 4, 1, "s"),
-    ("Mpe", 5, 0),
-    ("SWex", 0, "v"),
-    ("Mpe", 5, 1),
-    ("Mex", 5, 0, "s"),
-    ("Hq", 4),
-    ("Mv", 4),
-    ("Mpe", 6, 0),
-    ("Mex", 5, 1, "s"),
-    ("Mpe", 6, 1),
-    ("Mex", 6, 0, "s"),
-    ("Hq", 5),
-    ("Mv", 5),
-    ("Mpe", 7, 0),
-    ("Mex", 6, 1, "s"),
-    ("Mpe", 7, 1),
-    ("Mex", 7, 0, "s"),
-    ("Hq", 6),
-    ("Mv", 6),
-    ("Mex", 7, 1, "s"),
-    ("Hq", 7, 0),
-    ("Mv", 7, 0),
-    ("Hq", 7, 1),
-    ("Mv", 7, 1),
-    ("TWpe", 0),
-    ("TWpe", 1),
-    ("TWmul", 0),
-    ("SWpe", 4),
-    ("SWpe", 5),
-    ("SWpe", 6),
-    ("SWpe", 7),
-    ("TWmul", 1),
-    ("SWex", 1, "s"),
-    ("TWred",),
-)
+FRAMES = 8
+FEATURES = 1024
+LATENT = 512
+PACK = 4
+PASSES = FEATURES // (P * PACK)
+BANK = 512
+GROUP = 16
+GROUPS = P // GROUP
+THETA = 0
+PHI = 1
+FLOPS = 2 * (FRAMES * P) * FEATURES * (2 * LATENT) + 2 * FRAMES * P * P * LATENT + 2 * P * FRAMES * FRAMES * LATENT
+
+VECTOR_EMPTIES = (("phi", 0), ("phi", 3), ("x", 4), ("x", 7))
+WARM_BEFORE = 5
 
 
 def tile_higcin_volleyball_pa_kernel(tc, x, Wtheta, Wphi, out_0, out_1):
@@ -151,198 +36,199 @@ def tile_higcin_volleyball_pa_kernel(tc, x, Wtheta, Wphi, out_0, out_1):
         raw = ctx.enter_context(tc.tile_pool(name="raw", bufs=1))
         keep = ctx.enter_context(tc.tile_pool(name="keep", bufs=1))
         stage = ctx.enter_context(tc.tile_pool(name="stage", bufs=6))
-        tp_pool = ctx.enter_context(tc.psum_pool(name="tp", bufs=3))
-        mm_pool = ctx.enter_context(tc.psum_pool(name="mm", bufs=4))
-        sw_pool = ctx.enter_context(tc.psum_pool(name="swp", bufs=1))
+        flip_banks = ctx.enter_context(tc.psum_pool(name="flip", bufs=3))
+        proj_banks = ctx.enter_context(tc.psum_pool(name="proj", bufs=4))
+        first_bank = ctx.enter_context(tc.psum_pool(name="first", bufs=1))
 
-        w_dram = (
-            Wtheta.rearrange("(p t) d -> p t d", t=4),
-            Wphi.rearrange("(p t) d -> p t d", t=4),
-        )
-        src = {}
+        theta_tiles = [("theta", i) for i in range(PACK)]
+        phi_tiles = [("phi", i) for i in range(PACK)]
+        x_tiles = [("x", f) for f in range(FRAMES)]
+
+        dram = {}
+        for i in range(PACK):
+            dram[("theta", i)] = Wtheta.rearrange("(p i) d -> p i d", i=PACK)[:, i, :]
+            dram[("phi", i)] = Wphi.rearrange("(p i) d -> p i d", i=PACK)[:, i, :]
+        for f in range(FRAMES):
+            dram[("x", f)] = x[0, f]
+        rows = {}
         codes = {}
-        planes = {}
-        for u in LOADS:
-            src[u] = raw.tile([P, D], BF16, name="raw_" + u)
-            codes[u] = keep.tile([P, 256], U32, name="q_" + u, align_bytes=64)
-            planes[u] = keep.tile([P, 256], U8, name="s_" + u, align_bytes=64)
-            k = int(u[-1])
-            if u[0] == "x":
-                nc.sync.dma_start(out=src[u][:], in_=x[0, k])
-            else:
-                nc.sync.dma_start(out=src[u][:], in_=w_dram[0 if u[1] == "t" else 1][:, k, :])
+        scales = {}
+        for key in theta_tiles + x_tiles[0:3] + phi_tiles + x_tiles[3:8]:
+            label = "%s%d" % key
+            rows[key] = raw.tile([P, FEATURES], BF16, name="rows_" + label)
+            codes[key] = keep.tile([P, PASSES * P], U32, name="codes_" + label, align_bytes=64)
+            scales[key] = keep.tile([P, PASSES * P], U8, name="scales_" + label, align_bytes=64)
+            nc.sync.dma_start(out=rows[key][:], in_=dram[key])
 
-        zb = keep.tile([P, 512], BF16, name="zb")
-        nc.vector.memset(zb[:], 0.0)
-        scr = keep.tile([P, 1], F32, name="scr")
-        nc.scalar.mul(out=scr[:], in_=zb[:, 0:1], mul=1.0)
+        zeros = keep.tile([P, BANK], BF16, name="zeros")
+        nc.vector.memset(zeros[:], 0.0)
+        table_load = keep.tile([P, 1], F32, name="table_load")
+        nc.scalar.mul(out=table_load[:], in_=zeros[:, 0:1], mul=1.0)
         ident = keep.tile([P, P], F32, name="ident")
         make_identity(nc, ident[:])
-        hq = [keep.tile([P, 256], U32, name="hq%d" % f, align_bytes=64) for f in range(T)]
-        hs = [keep.tile([P, 256], U8, name="hs%d" % f, align_bytes=64) for f in range(T)]
-        for f in range(T):
-            nc.vector.memset(hs[f][:].bitcast(I32), 0)
-        m16raw = keep.tile([P, 16], F32, name="m16raw")
+        h_codes = [keep.tile([P, 2 * P], U32, name="h_codes%d" % f, align_bytes=64) for f in range(FRAMES)]
+        h_scales = [keep.tile([P, 2 * P], U8, name="h_scales%d" % f, align_bytes=64) for f in range(FRAMES)]
+        for f in range(FRAMES):
+            nc.vector.memset(h_scales[f][:].bitcast(I32), 0)
+        block_sum = keep.tile([P, GROUP], F32, name="block_sum")
         nc.vector.tensor_reduce(
-            out=m16raw[:], in_=ident[:].rearrange("p (t j) -> p j t", j=16), axis=AX.X, op=ALU.add
+            out=block_sum[:], in_=ident[:].rearrange("p (t j) -> p j t", j=GROUP), axis=AX.X, op=ALU.add
         )
-        m16 = keep.tile([P, 16], F32, name="m16")
-        nc.vector.tensor_scalar_mul(out=m16[:], in0=m16raw[:], scalar1=1.0 / T)
-        tq = keep.tile([P, 2048], U32, name="tq", align_bytes=64)
-        ts = keep.tile([P, 2048], U8, name="ts", align_bytes=64)
-        tq_v = tq[:].bitcast(I32).rearrange("p (g w t j) -> p g w t j", g=8, w=2, t=T)
-        ts_v = ts[:].bitcast(I32).rearrange("p (g w t j) -> p g w t j", g=8, w=2, t=T)
-        res = keep.tile([P, 64], F32, name="res")
-        prod = keep.tile([P, 64, 16], F32, name="prod")
+        same_node = keep.tile([P, GROUP], F32, name="same_node")
+        nc.vector.tensor_scalar_mul(out=same_node[:], in0=block_sum[:], scalar1=1.0 / FRAMES)
+        g_codes = keep.tile([P, GROUPS * 2 * P], U32, name="g_codes", align_bytes=64)
+        g_scales = keep.tile([P, GROUPS * 2 * P], U8, name="g_scales", align_bytes=64)
+        g_codes_view = g_codes[:].bitcast(I32).rearrange("p (g w t j) -> p g w t j", g=GROUPS, w=2, t=FRAMES)
+        g_scales_view = g_scales[:].bitcast(I32).rearrange("p (g w t j) -> p g w t j", g=GROUPS, w=2, t=FRAMES)
+        masked = keep.tile([P, GROUPS * FRAMES, GROUP], F32, name="masked")
+        tw_rows = keep.tile([P, GROUPS * FRAMES], F32, name="tw_rows")
+        warm_bank = first_bank.tile([P, BANK], F32, tag="first", name="warm_bank")
 
-        warm = sw_pool.tile([P, 512], F32, tag="sw", name="warm")
+        def warm_up():
+            nc.tensor.matmul(out=warm_bank[:], lhsT=zeros[:, 0:P], rhs=zeros[:], start=True, stop=True)
 
-        def Dm(cols, n=1):
-            for i in range(n):
-                nc.tensor.matmul(out=warm[:, 0:cols], lhsT=zb[:, 0:128], rhs=zb[:, 0:cols], start=True, stop=True)
+        def transpose_run(keys, warm=False):
+            copied = []
+            for key in keys:
+                bank = flip_banks.tile([P, PASSES, 2, P], F32, tag="flip", name="bank")
+                words = rows[key][:].bitcast(F32)
+                for c in range(PASSES):
+                    for h in range(2):
+                        first = (2 * c + h) * P
+                        nc.tensor.transpose(bank[:, c, h, :], words[:, first : first + P], ident[:])
+                if warm:
+                    warm_up()
+                grouped = stage.tile([P, FEATURES], BF16, tag="grouped", name="grouped", align_bytes=64)
+                target = grouped[:].bitcast(F32).rearrange("p (c r h) -> p c r h", c=PASSES, h=2)
+                source = bank[:].rearrange("p c h r -> p c r h")
+                if key in VECTOR_EMPTIES:
+                    nc.vector.tensor_copy(out=target, in_=source)
+                else:
+                    nc.scalar.copy(out=target, in_=source)
+                copied.append((key, grouped))
+                if len(copied) > 1:
+                    quantise_tile(*copied[-2])
+            quantise_tile(*copied[-1])
 
-        banks = {}
-        grouped = {}
-        accs = {}
-        hgrp = {}
-        sw_acc = {}
-        tw_acc = {}
+        def quantise_tile(key, grouped):
+            nc.vector.quantize_mx(out=codes[key][:].bitcast(FP8X4), scales=scales[key][:], in_=grouped[:])
 
-        def copy_out(eng, out, in_):
-            if eng == "s":
-                nc.scalar.copy(out=out, in_=in_)
-            else:
-                nc.vector.tensor_copy(out=out, in_=in_)
+        h_grouped = {}
+        unmoved = {}
 
-        def Tpe(u):
-            banks[u] = tp_pool.tile([P, 2, 2, P], F32, tag="tp", name="bank")
-            words = src[u][:].bitcast(F32)
-            for g in range(2):
-                for h in range(2):
-                    c0 = 256 * g + 128 * h
-                    nc.tensor.transpose(banks[u][:, g, h, :], words[:, c0 : c0 + 128], ident[:])
+        def project_run(pairs):
+            for f, w in pairs:
+                bank = proj_banks.tile([P, PACK, P], F32, tag="proj", name="bank")
+                for i in range(PACK):
+                    weight = (("theta", i), ("phi", i))[w]
+                    for c in range(PASSES):
+                        cols = slice(c * P, (c + 1) * P)
+                        nc.tensor.matmul_mx(
+                            out=bank[:, i, :],
+                            lhsT=codes[weight][:, cols].bitcast(FP8X4),
+                            lhsT_scale=scales[weight][:, cols],
+                            rhs=codes[("x", f)][:, cols].bitcast(FP8X4),
+                            rhs_scale=scales[("x", f)][:, cols],
+                            start=(c == 0),
+                            stop=(c == PASSES - 1),
+                        )
+                if f not in h_grouped:
+                    h_grouped[f] = stage.tile([P, 2, P, PACK], BF16, tag="h_grouped", name="h_grouped", align_bytes=64)
+                nc.scalar.copy(out=h_grouped[f][:, w, :, :], in_=bank[:].rearrange("p i r -> p r i"))
+                if f == FRAMES - 1:
+                    quantise_h(f, w, w + 1)
+                elif w == PHI:
+                    quantise_h(f, THETA, PHI + 1)
 
-        def Tex(u, eng):
-            grouped[u] = stage.tile([P, 1024], BF16, tag="grouped", name="grouped", align_bytes=64)
-            copy_out(
-                eng,
-                grouped[u][:].bitcast(F32).rearrange("p (g r h) -> p g r h", g=2, h=2),
-                banks[u][:].rearrange("p g h r -> p g r h"),
+        def quantise_h(f, w_from, w_to):
+            cols = slice(w_from * P, w_to * P)
+            nc.vector.quantize_mx(
+                out=h_codes[f][:, cols].bitcast(FP8X4),
+                scales=h_scales[f][:, cols],
+                in_=h_grouped[f][:, w_from:w_to, :, :].rearrange("p w r i -> p (w r i)"),
             )
+            move_unmoved()
+            unmoved["piece"] = (f, w_from, w_to)
 
-        def Tq(u):
-            nc.vector.quantize_mx(out=codes[u][:].bitcast(FP8X4), scales=planes[u][:], in_=grouped[u][:])
-
-        def Mpe(f, w, tiles=(0, 1, 2, 3)):
-            if (f, w) not in accs:
-                accs[(f, w)] = mm_pool.tile([P, 4, P], F32, tag="mm", name="acc")
-            xu = "x%d" % f
-            for t in tiles:
-                wu = ("wt%d" if w == 0 else "wp%d") % t
-                for g in range(2):
-                    cols = slice(128 * g, 128 * g + 128)
-                    nc.tensor.matmul_mx(
-                        out=accs[(f, w)][:, t, :],
-                        lhsT=codes[wu][:, cols].bitcast(FP8X4),
-                        lhsT_scale=planes[wu][:, cols],
-                        rhs=codes[xu][:, cols].bitcast(FP8X4),
-                        rhs_scale=planes[xu][:, cols],
-                        start=(g == 0),
-                        stop=(g == 1),
-                    )
-
-        def Mex(f, w, eng):
-            if f not in hgrp:
-                hgrp[f] = stage.tile([P, 2, P, 4], BF16, tag="hgrp", name="hgrp", align_bytes=64)
-            copy_out(eng, hgrp[f][:, w, :, :], accs[(f, w)][:].rearrange("p t r -> p r t"))
-
-        def Hq(f, w=None):
-            if w is None:
-                nc.vector.quantize_mx(
-                    out=hq[f][:].bitcast(FP8X4), scales=hs[f][:], in_=hgrp[f][:].rearrange("p w r t -> p (w r t)")
-                )
-            else:
-                cols = slice(128 * w, 128 * w + 128)
-                nc.vector.quantize_mx(
-                    out=hq[f][:, cols].bitcast(FP8X4),
-                    scales=hs[f][:, cols],
-                    in_=hgrp[f][:, w, :, :].rearrange("p r t -> p (r t)"),
-                )
-
-        def Mv(f, w=None):
-            if w is None:
+        def move_unmoved():
+            if "piece" not in unmoved:
+                return
+            f, w_from, w_to = unmoved["piece"]
+            for plain, by_group, run in ((h_codes, g_codes_view, GROUP), (h_scales, g_scales_view, GROUP // 4)):
                 nc.vector.tensor_copy(
-                    out=tq_v[:, :, :, f, :], in_=hq[f][:].bitcast(I32).rearrange("p (w g j) -> p g w j", w=2, g=8)
-                )
-                nc.vector.tensor_copy(
-                    out=ts_v[:, :, :, f, :], in_=hs[f][:].bitcast(I32).rearrange("p (w g j) -> p g w j", w=2, g=8)
-                )
-            else:
-                nc.vector.tensor_copy(
-                    out=tq_v[:, :, w, f, :],
-                    in_=hq[f][:].bitcast(I32)[:, 128 * w : 128 * w + 128].rearrange("p (g j) -> p g j", g=8),
-                )
-                nc.vector.tensor_copy(
-                    out=ts_v[:, :, w, f, :],
-                    in_=hs[f][:].bitcast(I32)[:, 32 * w : 32 * w + 32].rearrange("p (g j) -> p g j", g=8),
+                    out=by_group[:, :, w_from:w_to, f, :],
+                    in_=plain[f][:]
+                    .bitcast(I32)[:, w_from * GROUPS * run : w_to * GROUPS * run]
+                    .rearrange("p (w g j) -> p g w j", g=GROUPS, j=run),
                 )
 
-        def SWpe(f):
-            h = f // 4
-            if h not in sw_acc:
-                sw_acc[h] = sw_pool.tile([P, 4, P], F32, tag="sw", name="swacc")
+        def spatial(bank, f):
             nc.tensor.matmul_mx(
-                out=sw_acc[h][:, f % 4, :],
-                lhsT=hq[f][:, 0:128].bitcast(FP8X4),
-                lhsT_scale=hs[f][:, 0:128],
-                rhs=hq[f][:, 128:256].bitcast(FP8X4),
-                rhs_scale=hs[f][:, 128:256],
+                out=bank[:, f % 4, :],
+                lhsT=h_codes[f][:, 0:P].bitcast(FP8X4),
+                lhsT_scale=h_scales[f][:, 0:P],
+                rhs=h_codes[f][:, P : 2 * P].bitcast(FP8X4),
+                rhs_scale=h_scales[f][:, P : 2 * P],
                 start=True,
                 stop=True,
             )
 
-        def SWex(h, eng):
-            sw_sb = stage.tile([P, 4, P], F32, tag="sw_sb", name="sw_sb")
-            if eng == "s":
-                nc.scalar.mul(out=sw_sb[:], in_=sw_acc[h][:], mul=1.0 / N)
-            else:
-                nc.vector.tensor_scalar_mul(out=sw_sb[:], in0=sw_acc[h][:], scalar1=1.0 / N)
-            nc.sync.dma_start(out=out_0[0, 4 * h : 4 * h + 4].rearrange("t j k -> j t k"), in_=sw_sb[:])
+        def store_spatial(bank, f_from):
+            sw_rows = stage.tile([P, 4, P], F32, tag="sw_rows", name="sw_rows")
+            nc.scalar.mul(out=sw_rows[:], in_=bank[:], mul=1.0 / P)
+            nc.sync.dma_start(out=out_0[0, f_from : f_from + 4].rearrange("t j k -> j t k"), in_=sw_rows[:])
 
-        def TWpe(h):
-            tw_acc[h] = tp_pool.tile([P, 4, P], F32, tag="tp", name="twacc")
-            for gg in range(4):
-                c0 = 256 * (4 * h + gg)
+        def temporal(half):
+            bank = flip_banks.tile([P, 4, P], F32, tag="flip", name="bank")
+            for i in range(4):
+                first = (4 * half + i) * 2 * P
                 nc.tensor.matmul_mx(
-                    out=tw_acc[h][:, gg, :],
-                    lhsT=tq[:, c0 : c0 + 128].bitcast(FP8X4),
-                    lhsT_scale=ts[:, c0 : c0 + 128],
-                    rhs=tq[:, c0 + 128 : c0 + 256].bitcast(FP8X4),
-                    rhs_scale=ts[:, c0 + 128 : c0 + 256],
+                    out=bank[:, i, :],
+                    lhsT=g_codes[:, first : first + P].bitcast(FP8X4),
+                    lhsT_scale=g_scales[:, first : first + P],
+                    rhs=g_codes[:, first + P : first + 2 * P].bitcast(FP8X4),
+                    rhs_scale=g_scales[:, first + P : first + 2 * P],
                     start=True,
                     stop=True,
                 )
+            return bank
 
-        def TWmul(h):
+        def keep_same_node(bank, half):
             nc.vector.tensor_tensor(
-                out=prod[:, 32 * h : 32 * h + 32, :],
-                in0=tw_acc[h][:].rearrange("p g (s j) -> p (g s) j", j=16),
-                in1=m16[:].unsqueeze(1).to_broadcast([P, 32, 16]),
+                out=masked[:, 32 * half : 32 * half + 32, :],
+                in0=bank[:].rearrange("p g (s j) -> p (g s) j", j=GROUP),
+                in1=same_node[:].unsqueeze(1).to_broadcast([P, 32, GROUP]),
                 op=ALU.mult,
             )
 
-        def TWred():
-            nc.vector.tensor_reduce(out=res[:], in_=prod[:], axis=AX.X, op=ALU.add)
-            for t in range(T):
-                q = nc.sync if t % 2 == 0 else nc.scalar
-                q.dma_start(
-                    out=out_1[0, t].rearrange("(g j) s -> j g s", j=16),
-                    in_=res[16 * t : 16 * t + 16, :].rearrange("p (g s) -> p g s", s=8),
-                )
+        for i in range(WARM_BEFORE):
+            warm_up()
+        transpose_run(theta_tiles + x_tiles[0:3], warm=True)
+        project_run([(0, THETA), (1, THETA)])
+        transpose_run(phi_tiles)
+        project_run([(2, THETA)])
+        transpose_run(x_tiles[3:6])
+        project_run([(0, PHI), (1, PHI), (2, PHI), (3, THETA), (3, PHI)])
+        transpose_run(x_tiles[6:8])
+        project_run([(f, w) for f in range(4, FRAMES) for w in (THETA, PHI)])
+        move_unmoved()
 
-        table = {
-            "Tpe": Tpe, "Tex": Tex, "Tq": Tq, "Mpe": Mpe, "Mex": Mex, "Hq": Hq, "Mv": Mv,
-            "SWpe": SWpe, "Dm": Dm, "SWex": SWex, "TWpe": TWpe, "TWmul": TWmul, "TWred": TWred,
-        }
-        for step in STEPS:
-            table[step[0]](*step[1:])
+        sw_early = first_bank.tile([P, 4, P], F32, tag="first", name="sw_early")
+        sw_late = proj_banks.tile([P, 4, P], F32, tag="proj", name="sw_late")
+        for f in range(4):
+            spatial(sw_early, f)
+        store_spatial(sw_early, 0)
+        for f in range(4, FRAMES - 1):
+            spatial(sw_late, f)
+        tw_banks = [temporal(0), temporal(1)]
+        spatial(sw_late, FRAMES - 1)
+        keep_same_node(tw_banks[0], 0)
+        store_spatial(sw_late, 4)
+        keep_same_node(tw_banks[1], 1)
+        nc.vector.tensor_reduce(out=tw_rows[:], in_=masked[:], axis=AX.X, op=ALU.add)
+        for t in range(FRAMES):
+            queue = nc.sync if t % 2 == 0 else nc.scalar
+            queue.dma_start(
+                out=out_1[0, t].rearrange("(g j) s -> j g s", j=GROUP),
+                in_=tw_rows[GROUP * t : GROUP * (t + 1), :].rearrange("p (g s) -> p g s", s=FRAMES),
+            )

@@ -227,8 +227,7 @@ def tile_higcin_volleyball_pa_kernel(tc, x, Wtheta, Wphi, out_0, out_1):
         keep_same_node(tw_banks[1], 1)
         nc.vector.tensor_reduce(out=tw_rows[:], in_=masked[:], axis=AX.X, op=ALU.add)
         for t in range(FRAMES):
-            queue = nc.sync if t % 2 == 0 else nc.scalar
-            queue.dma_start(
+            nc.sync.dma_start(
                 out=out_1[0, t].rearrange("(g j) s -> j g s", j=GROUP),
                 in_=tw_rows[GROUP * t : GROUP * (t + 1), :].rearrange("p (g s) -> p g s", s=FRAMES),
             )

from contextlib import ExitStack

import concourse.mybir as mybir
from concourse.masks import make_identity

F32 = mybir.dt.float32
BF16 = mybir.dt.bfloat16
U32 = mybir.dt.uint32
I32 = mybir.dt.int32
U8 = mybir.dt.uint8
FP8X4 = mybir.dt.float8_e4m3fn_x4
ALU = mybir.AluOpType
AX = mybir.AxisListType

P = 128
FRAMES = 8
FEATURES = 1024
LATENT = 512
PACK = 4
PASSES = FEATURES // (P * PACK)
BANK = 512
GROUP = 16
GROUPS = P // GROUP
THETA = 0
PHI = 1
FLOPS = 2 * (FRAMES * P) * FEATURES * (2 * LATENT) + 2 * FRAMES * P * P * LATENT + 2 * P * FRAMES * FRAMES * LATENT

VECTOR_EMPTIES = (("phi", 0), ("phi", 3), ("x", 4), ("x", 7))
WARM_BEFORE = 5


def tile_higcin_volleyball_pa_kernel(tc, x, Wtheta, Wphi, out_0, out_1):
    nc = tc.nc
    with ExitStack() as ctx:
        ctx.enter_context(tc.manual_schedule())
        raw = ctx.enter_context(tc.tile_pool(name="raw", bufs=1))
        keep = ctx.enter_context(tc.tile_pool(name="keep", bufs=1))
        stage = ctx.enter_context(tc.tile_pool(name="stage", bufs=6))
        flip_banks = ctx.enter_context(tc.psum_pool(name="flip", bufs=3))
        proj_banks = ctx.enter_context(tc.psum_pool(name="proj", bufs=4))
        first_bank = ctx.enter_context(tc.psum_pool(name="first", bufs=1))

        theta_tiles = [("theta", i) for i in range(PACK)]
        phi_tiles = [("phi", i) for i in range(PACK)]
        x_tiles = [("x", f) for f in range(FRAMES)]

        dram = {}
        for i in range(PACK):
            dram[("theta", i)] = Wtheta.rearrange("(p i) d -> p i d", i=PACK)[:, i, :]
            dram[("phi", i)] = Wphi.rearrange("(p i) d -> p i d", i=PACK)[:, i, :]
        for f in range(FRAMES):
            dram[("x", f)] = x[0, f]
        rows = {}
        codes = {}
        scales = {}
        for key in theta_tiles + x_tiles[0:3] + phi_tiles + x_tiles[3:8]:
            label = "%s%d" % key
            rows[key] = raw.tile([P, FEATURES], BF16, name="rows_" + label)
            codes[key] = keep.tile([P, PASSES * P], U32, name="codes_" + label, align_bytes=64)
            scales[key] = keep.tile([P, PASSES * P], U8, name="scales_" + label, align_bytes=64)
            nc.sync.dma_start(out=rows[key][:], in_=dram[key])

        zeros = keep.tile([P, BANK], BF16, name="zeros")
        nc.vector.memset(zeros[:], 0.0)
        table_load = keep.tile([P, 1], F32, name="table_load")
        nc.scalar.mul(out=table_load[:], in_=zeros[:, 0:1], mul=1.0)
        ident = keep.tile([P, P], F32, name="ident")
        make_identity(nc, ident[:])
        h_codes = [keep.tile([P, 2 * P], U32, name="h_codes%d" % f, align_bytes=64) for f in range(FRAMES)]
        h_scales = [keep.tile([P, 2 * P], U8, name="h_scales%d" % f, align_bytes=64) for f in range(FRAMES)]
        for f in range(FRAMES):
            nc.vector.memset(h_scales[f][:].bitcast(I32), 0)
        block_sum = keep.tile([P, GROUP], F32, name="block_sum")
        nc.vector.tensor_reduce(
            out=block_sum[:], in_=ident[:].rearrange("p (t j) -> p j t", j=GROUP), axis=AX.X, op=ALU.add
        )
        same_node = keep.tile([P, GROUP], F32, name="same_node")
        nc.vector.tensor_scalar_mul(out=same_node[:], in0=block_sum[:], scalar1=1.0 / FRAMES)
        g_codes = keep.tile([P, GROUPS * 2 * P], U32, name="g_codes", align_bytes=64)
        g_scales = keep.tile([P, GROUPS * 2 * P], U8, name="g_scales", align_bytes=64)
        g_codes_view = g_codes[:].bitcast(I32).rearrange("p (g w t j) -> p g w t j", g=GROUPS, w=2, t=FRAMES)
        g_scales_view = g_scales[:].bitcast(I32).rearrange("p (g w t j) -> p g w t j", g=GROUPS, w=2, t=FRAMES)
        masked = keep.tile([P, GROUPS * FRAMES, GROUP], F32, name="masked")
        tw_rows = keep.tile([P, GROUPS * FRAMES], F32, name="tw_rows")
        warm_bank = first_bank.tile([P, BANK], F32, tag="first", name="warm_bank")

        def warm_up():
            nc.tensor.matmul(out=warm_bank[:], lhsT=zeros[:, 0:P], rhs=zeros[:], start=True, stop=True)

        def transpose_run(keys, warm=False):
            copied = []
            for key in keys:
                bank = flip_banks.tile([P, PASSES, 2, P], F32, tag="flip", name="bank")
                words = rows[key][:].bitcast(F32)
                for c in range(PASSES):
                    for h in range(2):
                        first = (2 * c + h) * P
                        nc.tensor.transpose(bank[:, c, h, :], words[:, first : first + P], ident[:])
                if warm:
                    warm_up()
                grouped = stage.tile([P, FEATURES], BF16, tag="grouped", name="grouped", align_bytes=64)
                target = grouped[:].bitcast(F32).rearrange("p (c r h) -> p c r h", c=PASSES, h=2)
                source = bank[:].rearrange("p c h r -> p c r h")
                if key in VECTOR_EMPTIES:
                    nc.vector.tensor_copy(out=target, in_=source)
                else:
                    nc.scalar.copy(out=target, in_=source)
                copied.append((key, grouped))
                if len(copied) > 1:
                    quantise_tile(*copied[-2])
            quantise_tile(*copied[-1])

        def quantise_tile(key, grouped):
            nc.vector.quantize_mx(out=codes[key][:].bitcast(FP8X4), scales=scales[key][:], in_=grouped[:])

        h_grouped = {}
        unmoved = {}

        def project_run(pairs):
            for f, w in pairs:
                bank = proj_banks.tile([P, PACK, P], F32, tag="proj", name="bank")
                for i in range(PACK):
                    weight = (("theta", i), ("phi", i))[w]
                    for c in range(PASSES):
                        cols = slice(c * P, (c + 1) * P)
                        nc.tensor.matmul_mx(
                            out=bank[:, i, :],
                            lhsT=codes[weight][:, cols].bitcast(FP8X4),
                            lhsT_scale=scales[weight][:, cols],
                            rhs=codes[("x", f)][:, cols].bitcast(FP8X4),
                            rhs_scale=scales[("x", f)][:, cols],
                            start=(c == 0),
                            stop=(c == PASSES - 1),
                        )
                if f not in h_grouped:
                    h_grouped[f] = stage.tile([P, 2, P, PACK], BF16, tag="h_grouped", name="h_grouped", align_bytes=64)
                nc.scalar.copy(out=h_grouped[f][:, w, :, :], in_=bank[:].rearrange("p i r -> p r i"))
                if f == FRAMES - 1:
                    quantise_h(f, w, w + 1)
                elif w == PHI:
                    quantise_h(f, THETA, PHI + 1)

        def quantise_h(f, w_from, w_to):
            cols = slice(w_from * P, w_to * P)
            nc.vector.quantize_mx(
                out=h_codes[f][:, cols].bitcast(FP8X4),
                scales=h_scales[f][:, cols],
                in_=h_grouped[f][:, w_from:w_to, :, :].rearrange("p w r i -> p (w r i)"),
            )
            move_unmoved()
            unmoved["piece"] = (f, w_from, w_to)

        def move_unmoved():
            if "piece" not in unmoved:
                return
            f, w_from, w_to = unmoved["piece"]
            for plain, by_group, run in ((h_codes, g_codes_view, GROUP), (h_scales, g_scales_view, GROUP // 4)):
                nc.vector.tensor_copy(
                    out=by_group[:, :, w_from:w_to, f, :],
                    in_=plain[f][:]
                    .bitcast(I32)[:, w_from * GROUPS * run : w_to * GROUPS * run]
                    .rearrange("p (w g j) -> p g w j", g=GROUPS, j=run),
                )

        def spatial(bank, f):
            nc.tensor.matmul_mx(
                out=bank[:, f % 4, :],
                lhsT=h_codes[f][:, 0:P].bitcast(FP8X4),
                lhsT_scale=h_scales[f][:, 0:P],
                rhs=h_codes[f][:, P : 2 * P].bitcast(FP8X4),
                rhs_scale=h_scales[f][:, P : 2 * P],
                start=True,
                stop=True,
            )

        def store_spatial(bank, f_from):
            sw_rows = stage.tile([P, 4, P], F32, tag="sw_rows", name="sw_rows")
            nc.scalar.mul(out=sw_rows[:], in_=bank[:], mul=1.0 / P)
            nc.sync.dma_start(out=out_0[0, f_from : f_from + 4].rearrange("t j k -> j t k"), in_=sw_rows[:])

        def temporal(half):
            bank = flip_banks.tile([P, 4, P], F32, tag="flip", name="bank")
            for i in range(4):
                first = (4 * half + i) * 2 * P
                nc.tensor.matmul_mx(
                    out=bank[:, i, :],
                    lhsT=g_codes[:, first : first + P].bitcast(FP8X4),
                    lhsT_scale=g_scales[:, first : first + P],
                    rhs=g_codes[:, first + P : first + 2 * P].bitcast(FP8X4),
                    rhs_scale=g_scales[:, first + P : first + 2 * P],
                    start=True,
                    stop=True,
                )
            return bank

        def keep_same_node(bank, half):
            nc.vector.tensor_tensor(
                out=masked[:, 32 * half : 32 * half + 32, :],
                in0=bank[:].rearrange("p g (s j) -> p (g s) j", j=GROUP),
                in1=same_node[:].unsqueeze(1).to_broadcast([P, 32, GROUP]),
                op=ALU.mult,
            )

        for i in range(WARM_BEFORE):
            warm_up()
        transpose_run(theta_tiles + x_tiles[0:3], warm=True)
        project_run([(0, THETA), (1, THETA)])
        transpose_run(phi_tiles)
        project_run([(2, THETA)])
        transpose_run(x_tiles[3:6])
        project_run([(0, PHI), (1, PHI), (2, PHI), (3, THETA), (3, PHI)])
        transpose_run(x_tiles[6:8])
        project_run([(f, w) for f in range(4, FRAMES) for w in (THETA, PHI)])
        move_unmoved()

        sw_early = first_bank.tile([P, 4, P], F32, tag="first", name="sw_early")
        sw_late = proj_banks.tile([P, 4, P], F32, tag="proj", name="sw_late")
        for f in range(4):
            spatial(sw_early, f)
        store_spatial(sw_early, 0)
        for f in range(4, FRAMES - 1):
            spatial(sw_late, f)
        tw_banks = [temporal(0), temporal(1)]
        spatial(sw_late, FRAMES - 1)
        keep_same_node(tw_banks[0], 0)
        store_spatial(sw_late, 4)
        keep_same_node(tw_banks[1], 1)
        nc.vector.tensor_reduce(out=tw_rows[:], in_=masked[:], axis=AX.X, op=ALU.add)
        for t in range(FRAMES):
            nc.sync.dma_start(
                out=out_1[0, t].rearrange("(g j) s -> j g s", j=GROUP),
                in_=tw_rows[GROUP * t : GROUP * (t + 1), :].rearrange("p (g s) -> p g s", s=FRAMES),
            )
